import numpy as np
import ml_dtypes


def mxq(x, axis, fmt="e4m3"):
    dtype, down = {"e4m3": (ml_dtypes.float8_e4m3fn, 7), "e5m2": (ml_dtypes.float8_e5m2, 14)}[fmt]
    v = np.moveaxis(np.asarray(x, np.float32).astype(ml_dtypes.bfloat16).astype(np.float64), axis, -1)
    blocks = v.reshape(v.shape[:-1] + (-1, 32))
    amax = np.abs(blocks).max(-1, keepdims=True)
    byte = np.maximum(np.where(amax > 0, np.frexp(amax)[1] - 1 + 127, 0) - down, 1)
    scale = np.exp2(byte - 127.0)
    codes = (blocks / scale).astype(np.float32).astype(dtype).astype(np.float64)
    return np.moveaxis((codes * scale).reshape(v.shape), -1, axis)


WIDE = False


def mx_kscale(k):
    if not WIDE:
        return np.ones(k)
    levels = np.array([10, -10, 5, -5, 0])
    a = np.random.permutation(np.resize(levels, k // 512 * 4)).reshape(k // 512, 4)
    idx = np.arange(k)
    return np.exp2(a[idx // 512, idx % 128 // 32])


BF16 = ml_dtypes.bfloat16


def bf(x):
    return np.asarray(x, np.float32).astype(BF16)


def f64(x):
    return np.asarray(x).astype(np.float64)


E2M1 = np.array([0.0, 0.5, 1.0, 1.5, 2.0, 3.0, 4.0, 6.0, -0.0, -0.5, -1.0, -1.5, -2.0, -3.0, -4.0, -6.0])


def pack_weight(w, fmt):
    k, n = w.shape
    w = f64(bf(w)).reshape(k // 32, 32, n)
    amax = np.abs(w).max(1)
    if fmt == "e4m3":
        byte = np.frexp(amax)[1] - 1 + 127 - 7
    else:
        mant, ex = np.frexp(amax / 6.0)
        byte = np.where(mant > 0.5, ex, ex - 1) + 127
    byte = np.clip(np.where(amax > 0, byte, 1), 1, 254)
    scaled = (w * np.exp2(127.0 - byte)[:, None, :]).reshape(k, n).astype(np.float32)
    by_word = np.ascontiguousarray(scaled.reshape(k // 512, 128, 4, n).transpose(0, 1, 3, 2))
    if fmt == "e4m3":
        words = by_word.astype(ml_dtypes.float8_e4m3fn).view(np.uint8)
    else:
        c = by_word.astype(ml_dtypes.float4_e2m1fn).view(np.uint8) & 0xF
        words = c[..., 0::2] | (c[..., 1::2] << 4)
    return np.ascontiguousarray(words), np.ascontiguousarray(byte.astype(np.uint8).reshape(k // 512, 16, n))


def unpack_weight(words, scales, fmt):
    g, p, n, _ = words.shape
    if fmt == "e4m3":
        vals = np.ascontiguousarray(words).view(ml_dtypes.float8_e4m3fn).astype(np.float64)
    else:
        nib = np.empty((g, p, n, 4), np.uint8)
        nib[..., 0::2] = words & 0xF
        nib[..., 1::2] = words >> 4
        vals = E2M1[nib]
    vals = vals * np.repeat(np.exp2(scales.astype(np.float64) - 127.0), 8, axis=1)[..., None]
    return vals.transpose(0, 1, 3, 2).reshape(g * 512, n)


B, S, H, O, W = 8, 128, 1024, 2048, 8


def setup_inputs():
    s = mx_kscale(H)
    hidden_states = bf(np.random.standard_normal((B, S, H)) * s)
    gate_proj = np.random.standard_normal((O, H)) / np.sqrt(H) / s[None, :]
    words, scales = pack_weight(np.ascontiguousarray(gate_proj.T), "e4m3")
    return {"hidden_states": hidden_states,
            "gate_proj_words": words,
            "gate_proj_scales": scales,
            "world_size": W}


def reference(hidden_states, gate_proj_words, gate_proj_scales, world_size):
    wt = unpack_weight(gate_proj_words, gate_proj_scales, "e4m3")
    h = wt.shape[0]
    view = f64(hidden_states).reshape(-1, h)
    mm = mxq(view, 1, "e4m3") @ wt
    n, o = mm.shape
    out = mm.reshape(world_size, n // world_size, o).sum(axis=0)
    return out

@@ -1,0 +1,114 @@
+from contextlib import ExitStack
+
+import concourse.mybir as mybir
+from concourse.masks import make_identity
+
+F32 = mybir.dt.float32
+BF16 = mybir.dt.bfloat16
+I32 = mybir.dt.int32
+U32 = mybir.dt.uint32
+U8 = mybir.dt.uint8
+FP8X4 = mybir.dt.float8_e4m3fn_x4
+
+P = 128
+PACK = 4
+K_PASS = P * PACK
+CHUNKS = 8
+H = 1024
+O = 2048
+GROUPS = H // K_PASS
+N_TILE = 512
+N_TILES = O // N_TILE
+PAIRS = PACK // 2
+QUADRANTS = 4
+
+FLOPS = 2 * CHUNKS * P * H * O
+
+
+def tile_testmmrsmodel_kernel(
+    tc, hidden_states, gate_proj_words, gate_proj_scales, world_size, out
+):
+    nc = tc.nc
+    assert world_size == CHUNKS
+
+    with ExitStack() as ctx:
+        keep = ctx.enter_context(tc.tile_pool(name="keep", bufs=1))
+        chunk_pool = ctx.enter_context(tc.tile_pool(name="chunk_pool", bufs=CHUNKS))
+        w_pool = ctx.enter_context(tc.tile_pool(name="w_pool", bufs=N_TILES))
+        stage = ctx.enter_context(tc.tile_pool(name="stage", bufs=4))
+        turn_psum = ctx.enter_context(tc.psum_pool(name="turn_psum", bufs=4))
+        acc_psum = ctx.enter_context(tc.psum_pool(name="acc_psum", bufs=N_TILES))
+
+        identity = keep.tile([P, P], F32)
+        make_identity(nc, identity[:])
+
+        w_planes = keep.tile([P, O], U8, align_bytes=64)
+        nc.vector.memset(w_planes[:].bitcast(I32), 0)
+        for quadrant in range(QUADRANTS):
+            first = 32 * quadrant
+            nc.sync.dma_start(
+                out=w_planes[first : first + 4 * GROUPS, :].bitcast(I32),
+                in_=gate_proj_scales[:, 4 * quadrant : 4 * quadrant + 4, :].bitcast(I32),
+            )
+
+        x_rows = []
+        for r in range(CHUNKS):
+            rows = chunk_pool.tile([P, H], BF16, name="rows")
+            nc.sync.dma_start(out=rows[:], in_=hidden_states[r])
+            x_rows.append(rows)
+
+        words_in_dram = gate_proj_words.rearrange("g p n t -> p g (n t)")
+        w_words = []
+        for n in range(N_TILES):
+            words = w_pool.tile([P, GROUPS, N_TILE], U32, name="words", align_bytes=64)
+            nc.sync.dma_start(
+                out=words[:].bitcast(I32),
+                in_=words_in_dram[:, :, PACK * N_TILE * n : PACK * N_TILE * (n + 1)].bitcast(I32),
+            )
+            w_words.append(words)
+
+        x_codes = []
+        x_planes = []
+        for r in range(CHUNKS):
+            row_words = x_rows[r][:].bitcast(F32)
+            turned = turn_psum.tile([P, GROUPS * PAIRS, P], F32)
+            for g in range(GROUPS):
+                for u in range(PAIRS):
+                    first = (K_PASS // 2) * g + u
+                    nc.tensor.transpose(
+                        turned[:, PAIRS * g + u, :],
+                        row_words[:, first : (K_PASS // 2) * (g + 1) : PAIRS],
+                        identity[:],
+                    )
+            grouped = stage.tile([P, GROUPS * P * PACK], BF16, align_bytes=64)
+            nc.scalar.copy(
+                out=grouped[:].bitcast(F32).rearrange("p (g j u) -> p g j u", g=GROUPS, u=PAIRS),
+                in_=turned[:].rearrange("p (g u) j -> p g j u", u=PAIRS),
+            )
+            codes = chunk_pool.tile([P, GROUPS, P], U32, name="codes", align_bytes=64)
+            plane = chunk_pool.tile([P, GROUPS, P], U8, name="plane", align_bytes=64)
+            nc.vector.quantize_mx(
+                out=codes[:].rearrange("p g j -> p (g j)").bitcast(FP8X4),
+                scales=plane[:].rearrange("p g j -> p (g j)"),
+                in_=grouped[:],
+            )
+            x_codes.append(codes)
+            x_planes.append(plane)
+
+        for n in range(N_TILES):
+            n_cols = slice(N_TILE * n, N_TILE * (n + 1))
+            acc = acc_psum.tile([P, N_TILE], F32)
+            for r in range(CHUNKS):
+                for g in range(GROUPS):
+                    nc.tensor.matmul_mx(
+                        out=acc[:],
+                        lhsT=x_codes[r][:, g, :].bitcast(FP8X4),
+                        lhsT_scale=x_planes[r][:, g, :],
+                        rhs=w_words[n][:, g, :].bitcast(FP8X4),
+                        rhs_scale=w_planes[4 * g : P, n_cols],
+                        start=(r == 0 and g == 0),
+                        stop=(r == CHUNKS - 1 and g == GROUPS - 1),
+                    )
+            result = stage.tile([P, N_TILE], F32)
+            nc.vector.tensor_copy(out=result[:], in_=acc[:])
+            nc.sync.dma_start(out=out[:, n_cols], in_=result[:])

@@ -34,13 +34,19 @@ def tile_testmmrsmodel_kernel(
     with ExitStack() as ctx:
         keep = ctx.enter_context(tc.tile_pool(name="keep", bufs=1))
         chunk_pool = ctx.enter_context(tc.tile_pool(name="chunk_pool", bufs=CHUNKS))
-        w_pool = ctx.enter_context(tc.tile_pool(name="w_pool", bufs=N_TILES))
+        w_pool = ctx.enter_context(tc.tile_pool(name="w_pool", bufs=N_TILES * GROUPS))
         stage = ctx.enter_context(tc.tile_pool(name="stage", bufs=4))
         turn_psum = ctx.enter_context(tc.psum_pool(name="turn_psum", bufs=4))
         acc_psum = ctx.enter_context(tc.psum_pool(name="acc_psum", bufs=N_TILES))
 
         identity = keep.tile([P, P], F32)
         make_identity(nc, identity[:])
+
+        x_rows = []
+        for r in range(CHUNKS):
+            rows = chunk_pool.tile([P, H], BF16, name="rows")
+            nc.sync.dma_start(out=rows[:], in_=hidden_states[r])
+            x_rows.append(rows)
 
         w_planes = keep.tile([P, O], U8, align_bytes=64)
         nc.vector.memset(w_planes[:].bitcast(I32), 0)
@@ -51,21 +57,16 @@ def tile_testmmrsmodel_kernel(
                 in_=gate_proj_scales[:, 4 * quadrant : 4 * quadrant + 4, :].bitcast(I32),
             )
 
-        x_rows = []
-        for r in range(CHUNKS):
-            rows = chunk_pool.tile([P, H], BF16, name="rows")
-            nc.sync.dma_start(out=rows[:], in_=hidden_states[r])
-            x_rows.append(rows)
-
-        words_in_dram = gate_proj_words.rearrange("g p n t -> p g (n t)")
-        w_words = []
+        w_words = {}
         for n in range(N_TILES):
-            words = w_pool.tile([P, GROUPS, N_TILE], U32, name="words", align_bytes=64)
-            nc.sync.dma_start(
-                out=words[:].bitcast(I32),
-                in_=words_in_dram[:, :, PACK * N_TILE * n : PACK * N_TILE * (n + 1)].bitcast(I32),
-            )
-            w_words.append(words)
+            for g in range(GROUPS):
+                words = w_pool.tile([P, N_TILE], U32, name="words", align_bytes=64)
+                bytes_in_dram = gate_proj_words[g].rearrange("p n t -> p (n t)")
+                nc.sync.dma_start(
+                    out=words[:].bitcast(I32),
+                    in_=bytes_in_dram[:, PACK * N_TILE * n : PACK * N_TILE * (n + 1)].bitcast(I32),
+                )
+                w_words[(n, g)] = words
 
         x_codes = []
         x_planes = []
@@ -98,16 +99,16 @@ def tile_testmmrsmodel_kernel(
         for n in range(N_TILES):
             n_cols = slice(N_TILE * n, N_TILE * (n + 1))
             acc = acc_psum.tile([P, N_TILE], F32)
-            for r in range(CHUNKS):
-                for g in range(GROUPS):
+            for g in range(GROUPS):
+                for r in range(CHUNKS):
                     nc.tensor.matmul_mx(
                         out=acc[:],
                         lhsT=x_codes[r][:, g, :].bitcast(FP8X4),
                         lhsT_scale=x_planes[r][:, g, :],
-                        rhs=w_words[n][:, g, :].bitcast(FP8X4),
+                        rhs=w_words[(n, g)][:].bitcast(FP8X4),
                         rhs_scale=w_planes[4 * g : P, n_cols],
-                        start=(r == 0 and g == 0),
-                        stop=(r == CHUNKS - 1 and g == GROUPS - 1),
+                        start=(g == 0 and r == 0),
+                        stop=(g == GROUPS - 1 and r == CHUNKS - 1),
                     )
             result = stage.tile([P, N_TILE], F32)
             nc.vector.tensor_copy(out=result[:], in_=acc[:])

@@ -14,6 +14,7 @@ P = 128
 PACK = 4
 K_PASS = P * PACK
 CHUNKS = 8
+HALF = CHUNKS // 2
 H = 1024
 O = 2048
 GROUPS = H // K_PASS
@@ -35,19 +36,79 @@ def tile_testmmrsmodel_kernel(
         keep = ctx.enter_context(tc.tile_pool(name="keep", bufs=1))
         chunk_pool = ctx.enter_context(tc.tile_pool(name="chunk_pool", bufs=CHUNKS))
         w_pool = ctx.enter_context(tc.tile_pool(name="w_pool", bufs=N_TILES * GROUPS))
-        stage = ctx.enter_context(tc.tile_pool(name="stage", bufs=4))
-        turn_psum = ctx.enter_context(tc.psum_pool(name="turn_psum", bufs=4))
+        stage = ctx.enter_context(tc.tile_pool(name="stage", bufs=HALF))
+        turn_psum = ctx.enter_context(tc.psum_pool(name="turn_psum", bufs=HALF))
         acc_psum = ctx.enter_context(tc.psum_pool(name="acc_psum", bufs=N_TILES))
+        ctx.enter_context(tc.manual_schedule())
+
+        x_rows = {}
+        x_sorted = {}
+        x_codes = {}
+        x_planes = {}
+        w_words = {}
+
+        def load_chunks(half):
+            for r in range(HALF * half, HALF * (half + 1)):
+                x_rows[r] = chunk_pool.tile([P, H], BF16, name="rows")
+                nc.sync.dma_start(out=x_rows[r][:], in_=hidden_states[r])
+
+        def load_w(n):
+            for g in range(GROUPS):
+                w_words[(n, g)] = w_pool.tile([P, N_TILE], U32, name="words", align_bytes=64)
+                bytes_in_dram = gate_proj_words[g].rearrange("p n t -> p (n t)")
+                nc.sync.dma_start(
+                    out=w_words[(n, g)][:].bitcast(I32),
+                    in_=bytes_in_dram[:, PACK * N_TILE * n : PACK * N_TILE * (n + 1)].bitcast(I32),
+                )
+
+        def quantise_chunks(half):
+            chunks = range(HALF * half, HALF * (half + 1))
+            for r in chunks:
+                x_sorted[r] = chunk_pool.tile([P, GROUPS, PAIRS, P], F32, name="sorted_words")
+                nc.vector.tensor_copy(
+                    out=x_sorted[r][:],
+                    in_=x_rows[r][:]
+                    .bitcast(F32)
+                    .rearrange("j (g p u) -> j g u p", g=GROUPS, u=PAIRS),
+                )
+            for r in chunks:
+                turned = turn_psum.tile([P, GROUPS, PAIRS, P], F32)
+                for g in range(GROUPS):
+                    for u in range(PAIRS):
+                        nc.tensor.transpose(turned[:, g, u, :], x_sorted[r][:, g, u, :], identity[:])
+                grouped = stage.tile([P, GROUPS * P * PACK], BF16, align_bytes=64)
+                nc.scalar.copy(
+                    out=grouped[:]
+                    .bitcast(F32)
+                    .rearrange("p (g j u) -> p g j u", g=GROUPS, u=PAIRS),
+                    in_=turned[:].rearrange("p g u j -> p g j u"),
+                )
+                x_codes[r] = chunk_pool.tile([P, GROUPS, P], U32, name="codes", align_bytes=64)
+                x_planes[r] = chunk_pool.tile([P, GROUPS, P], U8, name="plane", align_bytes=64)
+                nc.vector.quantize_mx(
+                    out=x_codes[r][:].rearrange("p g j -> p (g j)").bitcast(FP8X4),
+                    scales=x_planes[r][:].rearrange("p g j -> p (g j)"),
+                    in_=grouped[:],
+                )
+
+        def passes(half, n):
+            for g in range(GROUPS):
+                for r in range(HALF * half, HALF * (half + 1)):
+                    nc.tensor.matmul_mx(
+                        out=acc[n][:],
+                        lhsT=x_codes[r][:, g, :].bitcast(FP8X4),
+                        lhsT_scale=x_planes[r][:, g, :],
+                        rhs=w_words[(n, g)][:].bitcast(FP8X4),
+                        rhs_scale=w_planes[4 * g : P, N_TILE * n : N_TILE * (n + 1)],
+                        start=(g == 0 and r == 0),
+                        stop=(g == GROUPS - 1 and r == CHUNKS - 1),
+                    )
 
         identity = keep.tile([P, P], F32)
         make_identity(nc, identity[:])
+        acc = [acc_psum.tile([P, N_TILE], F32, name="acc") for n in range(N_TILES)]
 
-        x_rows = []
-        for r in range(CHUNKS):
-            rows = chunk_pool.tile([P, H], BF16, name="rows")
-            nc.sync.dma_start(out=rows[:], in_=hidden_states[r])
-            x_rows.append(rows)
-
+        load_chunks(0)
         w_planes = keep.tile([P, O], U8, align_bytes=64)
         nc.vector.memset(w_planes[:].bitcast(I32), 0)
         for quadrant in range(QUADRANTS):
@@ -56,60 +117,20 @@ def tile_testmmrsmodel_kernel(
                 out=w_planes[first : first + 4 * GROUPS, :].bitcast(I32),
                 in_=gate_proj_scales[:, 4 * quadrant : 4 * quadrant + 4, :].bitcast(I32),
             )
+        load_w(0)
+        load_w(1)
+        load_chunks(1)
+        load_w(2)
+        load_w(3)
 
-        w_words = {}
+        quantise_chunks(0)
+        passes(0, 0)
+        passes(0, 1)
+        quantise_chunks(1)
+        passes(0, 2)
+        passes(0, 3)
         for n in range(N_TILES):
-            for g in range(GROUPS):
-                words = w_pool.tile([P, N_TILE], U32, name="words", align_bytes=64)
-                bytes_in_dram = gate_proj_words[g].rearrange("p n t -> p (n t)")
-                nc.sync.dma_start(
-                    out=words[:].bitcast(I32),
-                    in_=bytes_in_dram[:, PACK * N_TILE * n : PACK * N_TILE * (n + 1)].bitcast(I32),
-                )
-                w_words[(n, g)] = words
-
-        x_codes = []
-        x_planes = []
-        for r in range(CHUNKS):
-            row_words = x_rows[r][:].bitcast(F32)
-            turned = turn_psum.tile([P, GROUPS * PAIRS, P], F32)
-            for g in range(GROUPS):
-                for u in range(PAIRS):
-                    first = (K_PASS // 2) * g + u
-                    nc.tensor.transpose(
-                        turned[:, PAIRS * g + u, :],
-                        row_words[:, first : (K_PASS // 2) * (g + 1) : PAIRS],
-                        identity[:],
-                    )
-            grouped = stage.tile([P, GROUPS * P * PACK], BF16, align_bytes=64)
-            nc.scalar.copy(
-                out=grouped[:].bitcast(F32).rearrange("p (g j u) -> p g j u", g=GROUPS, u=PAIRS),
-                in_=turned[:].rearrange("p (g u) j -> p g j u", u=PAIRS),
-            )
-            codes = chunk_pool.tile([P, GROUPS, P], U32, name="codes", align_bytes=64)
-            plane = chunk_pool.tile([P, GROUPS, P], U8, name="plane", align_bytes=64)
-            nc.vector.quantize_mx(
-                out=codes[:].rearrange("p g j -> p (g j)").bitcast(FP8X4),
-                scales=plane[:].rearrange("p g j -> p (g j)"),
-                in_=grouped[:],
-            )
-            x_codes.append(codes)
-            x_planes.append(plane)
-
-        for n in range(N_TILES):
-            n_cols = slice(N_TILE * n, N_TILE * (n + 1))
-            acc = acc_psum.tile([P, N_TILE], F32)
-            for g in range(GROUPS):
-                for r in range(CHUNKS):
-                    nc.tensor.matmul_mx(
-                        out=acc[:],
-                        lhsT=x_codes[r][:, g, :].bitcast(FP8X4),
-                        lhsT_scale=x_planes[r][:, g, :],
-                        rhs=w_words[(n, g)][:].bitcast(FP8X4),
-                        rhs_scale=w_planes[4 * g : P, n_cols],
-                        start=(g == 0 and r == 0),
-                        stop=(g == GROUPS - 1 and r == CHUNKS - 1),
-                    )
+            passes(1, n)
             result = stage.tile([P, N_TILE], F32)
-            nc.vector.tensor_copy(out=result[:], in_=acc[:])
-            nc.sync.dma_start(out=out[:, n_cols], in_=result[:])
+            nc.vector.tensor_copy(out=result[:], in_=acc[n][:])
+            nc.sync.dma_start(out=out[:, N_TILE * n : N_TILE * (n + 1)], in_=result[:])

@@ -76,6 +76,8 @@ def tile_testmmrsmodel_kernel(
                 for g in range(GROUPS):
                     for u in range(PAIRS):
                         nc.tensor.transpose(turned[:, g, u, :], x_sorted[r][:, g, u, :], identity[:])
+                if half == 0:
+                    spin(2, 256)
                 grouped = stage.tile([P, GROUPS * P * PACK], BF16, align_bytes=64)
                 nc.scalar.copy(
                     out=grouped[:]
@@ -91,6 +93,16 @@ def tile_testmmrsmodel_kernel(
                     in_=grouped[:],
                 )
 
+        def spin(count, width):
+            for i in range(count):
+                nc.tensor.matmul(
+                    out=acc[N_TILES - 1][:, 0:width],
+                    lhsT=zeros[:, 0:P],
+                    rhs=zeros[:, 0:width],
+                    start=True,
+                    stop=True,
+                )
+
         def passes(half, n):
             for g in range(GROUPS):
                 for r in range(HALF * half, HALF * (half + 1)):
@@ -104,9 +116,12 @@ def tile_testmmrsmodel_kernel(
                         stop=(g == GROUPS - 1 and r == CHUNKS - 1),
                     )
 
+        zeros = keep.tile([P, N_TILE], BF16)
+        nc.vector.memset(zeros[:], 0.0)
         identity = keep.tile([P, P], F32)
         make_identity(nc, identity[:])
         acc = [acc_psum.tile([P, N_TILE], F32, name="acc") for n in range(N_TILES)]
+        spin(5, N_TILE)
 
         load_chunks(0)
         w_planes = keep.tile([P, O], U8, align_bytes=64)

@@ -43,6 +43,7 @@ def tile_testmmrsmodel_kernel(
 
         x_rows = {}
         x_sorted = {}
+        x_grouped = {}
         x_codes = {}
         x_planes = {}
         w_words = {}
@@ -52,8 +53,8 @@ def tile_testmmrsmodel_kernel(
                 x_rows[r] = chunk_pool.tile([P, H], BF16, name="rows")
                 nc.sync.dma_start(out=x_rows[r][:], in_=hidden_states[r])
 
-        def load_w(n):
-            for g in range(GROUPS):
+        def load_w(n, groups):
+            for g in groups:
                 w_words[(n, g)] = w_pool.tile([P, N_TILE], U32, name="words", align_bytes=64)
                 bytes_in_dram = gate_proj_words[g].rearrange("p n t -> p (n t)")
                 nc.sync.dma_start(
@@ -61,37 +62,41 @@ def tile_testmmrsmodel_kernel(
                     in_=bytes_in_dram[:, PACK * N_TILE * n : PACK * N_TILE * (n + 1)].bitcast(I32),
                 )
 
-        def quantise_chunks(half):
-            chunks = range(HALF * half, HALF * (half + 1))
-            for r in chunks:
-                x_sorted[r] = chunk_pool.tile([P, GROUPS, PAIRS, P], F32, name="sorted_words")
-                nc.vector.tensor_copy(
-                    out=x_sorted[r][:],
-                    in_=x_rows[r][:]
-                    .bitcast(F32)
-                    .rearrange("j (g p u) -> j g u p", g=GROUPS, u=PAIRS),
-                )
-            for r in chunks:
-                turned = turn_psum.tile([P, GROUPS, PAIRS, P], F32)
-                for g in range(GROUPS):
-                    for u in range(PAIRS):
-                        nc.tensor.transpose(turned[:, g, u, :], x_sorted[r][:, g, u, :], identity[:])
-                if half == 0:
-                    spin(2, 256)
-                grouped = stage.tile([P, GROUPS * P * PACK], BF16, align_bytes=64)
-                nc.scalar.copy(
-                    out=grouped[:]
-                    .bitcast(F32)
-                    .rearrange("p (g j u) -> p g j u", g=GROUPS, u=PAIRS),
-                    in_=turned[:].rearrange("p g u j -> p g j u"),
-                )
-                x_codes[r] = chunk_pool.tile([P, GROUPS, P], U32, name="codes", align_bytes=64)
-                x_planes[r] = chunk_pool.tile([P, GROUPS, P], U8, name="plane", align_bytes=64)
-                nc.vector.quantize_mx(
-                    out=x_codes[r][:].rearrange("p g j -> p (g j)").bitcast(FP8X4),
-                    scales=x_planes[r][:].rearrange("p g j -> p (g j)"),
-                    in_=grouped[:],
-                )
+        def sort_words(r):
+            x_sorted[r] = chunk_pool.tile([P, GROUPS, PAIRS, P], F32, name="sorted_words")
+            nc.vector.tensor_copy(
+                out=x_sorted[r][:],
+                in_=x_rows[r][:]
+                .bitcast(F32)
+                .rearrange("j (g p u) -> j g u p", g=GROUPS, u=PAIRS),
+            )
+
+        def turn(r):
+            turned = turn_psum.tile([P, GROUPS, PAIRS, P], F32)
+            for g in range(GROUPS):
+                for u in range(PAIRS):
+                    if r in x_sorted:
+                        words = x_sorted[r][:, g, u, :]
+                    else:
+                        first = P * PAIRS * g + u
+                        words = x_rows[r][:].bitcast(F32)[:, first : P * PAIRS * (g + 1) : PAIRS]
+                    nc.tensor.transpose(turned[:, g, u, :], words, identity[:])
+            x_grouped[r] = stage.tile([P, GROUPS * P * PACK], BF16, name="grouped", align_bytes=64)
+            nc.scalar.copy(
+                out=x_grouped[r][:]
+                .bitcast(F32)
+                .rearrange("p (g j u) -> p g j u", g=GROUPS, u=PAIRS),
+                in_=turned[:].rearrange("p g u j -> p g j u"),
+            )
+
+        def quantise(r):
+            x_codes[r] = chunk_pool.tile([P, GROUPS, P], U32, name="codes", align_bytes=64)
+            x_planes[r] = chunk_pool.tile([P, GROUPS, P], U8, name="plane", align_bytes=64)
+            nc.vector.quantize_mx(
+                out=x_codes[r][:].rearrange("p g j -> p (g j)").bitcast(FP8X4),
+                scales=x_planes[r][:].rearrange("p g j -> p (g j)"),
+                in_=x_grouped[r][:],
+            )
 
         def spin(count, width):
             for i in range(count):
@@ -103,18 +108,29 @@ def tile_testmmrsmodel_kernel(
                     stop=True,
                 )
 
+        def one_pass(r, g, n):
+            nc.tensor.matmul_mx(
+                out=acc[n][:],
+                lhsT=x_codes[r][:, g, :].bitcast(FP8X4),
+                lhsT_scale=x_planes[r][:, g, :],
+                rhs=w_words[(n, g)][:].bitcast(FP8X4),
+                rhs_scale=w_planes[4 * g : P, N_TILE * n : N_TILE * (n + 1)],
+                start=(g == 0 and r == 0),
+                stop=(g == GROUPS - 1 and r == CHUNKS - 1),
+            )
+
         def passes(half, n):
             for g in range(GROUPS):
                 for r in range(HALF * half, HALF * (half + 1)):
-                    nc.tensor.matmul_mx(
-                        out=acc[n][:],
-                        lhsT=x_codes[r][:, g, :].bitcast(FP8X4),
-                        lhsT_scale=x_planes[r][:, g, :],
-                        rhs=w_words[(n, g)][:].bitcast(FP8X4),
-                        rhs_scale=w_planes[4 * g : P, N_TILE * n : N_TILE * (n + 1)],
-                        start=(g == 0 and r == 0),
-                        stop=(g == GROUPS - 1 and r == CHUNKS - 1),
-                    )
+                    one_pass(r, g, n)
+
+        def load_scales(first, last):
+            for quadrant in range(QUADRANTS):
+                top = 32 * quadrant
+                nc.sync.dma_start(
+                    out=w_planes[top : top + 4 * GROUPS, first:last].bitcast(I32),
+                    in_=gate_proj_scales[:, 4 * quadrant : 4 * quadrant + 4, first:last].bitcast(I32),
+                )
 
         zeros = keep.tile([P, N_TILE], BF16)
         nc.vector.memset(zeros[:], 0.0)
@@ -123,26 +139,30 @@ def tile_testmmrsmodel_kernel(
         acc = [acc_psum.tile([P, N_TILE], F32, name="acc") for n in range(N_TILES)]
         spin(5, N_TILE)
 
-        load_chunks(0)
         w_planes = keep.tile([P, O], U8, align_bytes=64)
         nc.vector.memset(w_planes[:].bitcast(I32), 0)
-        for quadrant in range(QUADRANTS):
-            first = 32 * quadrant
-            nc.sync.dma_start(
-                out=w_planes[first : first + 4 * GROUPS, :].bitcast(I32),
-                in_=gate_proj_scales[:, 4 * quadrant : 4 * quadrant + 4, :].bitcast(I32),
-            )
-        load_w(0)
-        load_w(1)
+        load_chunks(0)
+        load_scales(0, O)
+        load_w(0, (0, 1))
+        load_w(1, (0, 1))
+        load_w(2, (0, 1))
         load_chunks(1)
-        load_w(2)
-        load_w(3)
+        load_w(3, (0, 1))
 
-        quantise_chunks(0)
+        for r in range(HALF):
+            sort_words(r)
+        for r in range(HALF):
+            turn(r)
+            spin(2, 256)
+            quantise(r)
         passes(0, 0)
         passes(0, 1)
-        quantise_chunks(1)
         passes(0, 2)
+        for r in range(HALF, CHUNKS):
+            sort_words(r)
+        for r in range(HALF, CHUNKS):
+            turn(r)
+            quantise(r)
         passes(0, 3)
         for n in range(N_TILES):
             passes(1, n)

@@ -142,8 +142,10 @@ def tile_testmmrsmodel_kernel(
         w_planes = keep.tile([P, O], U8, align_bytes=64)
         nc.vector.memset(w_planes[:].bitcast(I32), 0)
         load_chunks(0)
-        load_scales(0, O)
-        load_w(0, (0, 1))
+        load_w(0, (0,))
+        load_scales(0, N_TILE)
+        load_w(0, (1,))
+        load_scales(N_TILE, O)
         load_w(1, (0, 1))
         load_w(2, (0, 1))
         load_chunks(1)

@@ -151,13 +151,25 @@ def tile_testmmrsmodel_kernel(
         load_chunks(1)
         load_w(3, (0, 1))
 
-        for r in range(HALF):
-            sort_words(r)
-        for r in range(HALF):
-            turn(r)
-            spin(2, 256)
-            quantise(r)
-        passes(0, 0)
+        sort_words(0)
+        sort_words(1)
+        turn(0)
+        spin(2, 256)
+        sort_words(2)
+        turn(1)
+        spin(2, 256)
+        quantise(0)
+        turn(2)
+        spin(2, 256)
+        quantise(1)
+        turn(3)
+        quantise(2)
+        quantise(3)
+        for g in range(GROUPS):
+            for r in range(HALF - 1):
+                one_pass(r, g, 0)
+        for g in range(GROUPS):
+            one_pass(HALF - 1, g, 0)
         passes(0, 1)
         passes(0, 2)
         for r in range(HALF, CHUNKS):

@@ -14,7 +14,8 @@ P = 128
 PACK = 4
 K_PASS = P * PACK
 CHUNKS = 8
-HALF = CHUNKS // 2
+DUO = 2
+DUOS = CHUNKS // DUO
 H = 1024
 O = 2048
 GROUPS = H // K_PASS
@@ -34,10 +35,10 @@ def tile_testmmrsmodel_kernel(
 
     with ExitStack() as ctx:
         keep = ctx.enter_context(tc.tile_pool(name="keep", bufs=1))
-        chunk_pool = ctx.enter_context(tc.tile_pool(name="chunk_pool", bufs=CHUNKS))
+        x_pool = ctx.enter_context(tc.tile_pool(name="x_pool", bufs=DUOS * GROUPS))
         w_pool = ctx.enter_context(tc.tile_pool(name="w_pool", bufs=N_TILES * GROUPS))
-        stage = ctx.enter_context(tc.tile_pool(name="stage", bufs=HALF))
-        turn_psum = ctx.enter_context(tc.psum_pool(name="turn_psum", bufs=HALF))
+        out_pool = ctx.enter_context(tc.tile_pool(name="out_pool", bufs=N_TILES))
+        turn_psum = ctx.enter_context(tc.psum_pool(name="turn_psum", bufs=4))
         acc_psum = ctx.enter_context(tc.psum_pool(name="acc_psum", bufs=N_TILES))
         ctx.enter_context(tc.manual_schedule())
 
@@ -47,55 +48,88 @@ def tile_testmmrsmodel_kernel(
         x_codes = {}
         x_planes = {}
         w_words = {}
+        w_planes = {}
 
-        def load_chunks(half):
-            for r in range(HALF * half, HALF * (half + 1)):
-                x_rows[r] = chunk_pool.tile([P, H], BF16, name="rows")
-                nc.sync.dma_start(out=x_rows[r][:], in_=hidden_states[r])
+        def load_x(duo, g):
+            x_rows[(duo, g)] = x_pool.tile([P, DUO, K_PASS], BF16, name="rows")
+            nc.sync.dma_start(
+                out=x_rows[(duo, g)][:],
+                in_=hidden_states[
+                    DUO * duo : DUO * (duo + 1), :, K_PASS * g : K_PASS * (g + 1)
+                ].rearrange("r j k -> j r k"),
+            )
+            x_grouped[(duo, g)] = x_pool.tile(
+                [P, DUO * P * PACK], BF16, name="grouped", align_bytes=64
+            )
+            x_codes[(duo, g)] = x_pool.tile([P, DUO, P], U32, name="codes", align_bytes=64)
+            x_planes[(duo, g)] = x_pool.tile([P, DUO, P], U8, name="plane", align_bytes=64)
 
-        def load_w(n, groups):
-            for g in groups:
-                w_words[(n, g)] = w_pool.tile([P, N_TILE], U32, name="words", align_bytes=64)
-                bytes_in_dram = gate_proj_words[g].rearrange("p n t -> p (n t)")
+        def load_w(n, g):
+            w_words[(n, g)] = w_pool.tile([P, N_TILE], U32, name="words", align_bytes=64)
+            bytes_in_dram = gate_proj_words[g].rearrange("p n t -> p (n t)")
+            nc.sync.dma_start(
+                out=w_words[(n, g)][:].bitcast(I32),
+                in_=bytes_in_dram[:, PACK * N_TILE * n : PACK * N_TILE * (n + 1)].bitcast(I32),
+            )
+
+        def load_scales(g):
+            for quadrant in range(QUADRANTS):
+                top = 32 * quadrant
                 nc.sync.dma_start(
-                    out=w_words[(n, g)][:].bitcast(I32),
-                    in_=bytes_in_dram[:, PACK * N_TILE * n : PACK * N_TILE * (n + 1)].bitcast(I32),
+                    out=w_planes[g][top : top + 4 * N_TILES, :].bitcast(I32),
+                    in_=gate_proj_scales[g, 4 * quadrant : 4 * quadrant + 4, :]
+                    .rearrange("s (n c) -> n s c", n=N_TILES)
+                    .bitcast(I32),
                 )
 
-        def sort_words(r):
-            x_sorted[r] = chunk_pool.tile([P, GROUPS, PAIRS, P], F32, name="sorted_words")
+        def sort_words(duo, g):
+            x_sorted[(duo, g)] = x_pool.tile([P, DUO, PAIRS, P], F32, name="sorted_words")
             nc.vector.tensor_copy(
-                out=x_sorted[r][:],
-                in_=x_rows[r][:]
-                .bitcast(F32)
-                .rearrange("j (g p u) -> j g u p", g=GROUPS, u=PAIRS),
+                out=x_sorted[(duo, g)][:],
+                in_=x_rows[(duo, g)][:].bitcast(F32).rearrange("j r (p u) -> j r u p", u=PAIRS),
             )
 
-        def turn(r):
-            turned = turn_psum.tile([P, GROUPS, PAIRS, P], F32)
-            for g in range(GROUPS):
+        def turn_duo(duo, g):
+            turned = turn_psum.tile([P, DUO, PAIRS, P], F32, name="turned")
+            for r in range(DUO):
                 for u in range(PAIRS):
-                    if r in x_sorted:
-                        words = x_sorted[r][:, g, u, :]
-                    else:
-                        first = P * PAIRS * g + u
-                        words = x_rows[r][:].bitcast(F32)[:, first : P * PAIRS * (g + 1) : PAIRS]
-                    nc.tensor.transpose(turned[:, g, u, :], words, identity[:])
-            x_grouped[r] = stage.tile([P, GROUPS * P * PACK], BF16, name="grouped", align_bytes=64)
+                    nc.tensor.transpose(
+                        turned[:, r, u, :], x_sorted[(duo, g)][:, r, u, :], identity[:]
+                    )
             nc.scalar.copy(
-                out=x_grouped[r][:]
+                out=x_grouped[(duo, g)][:]
                 .bitcast(F32)
-                .rearrange("p (g j u) -> p g j u", g=GROUPS, u=PAIRS),
-                in_=turned[:].rearrange("p g u j -> p g j u"),
+                .rearrange("p (r j u) -> p r j u", r=DUO, u=PAIRS),
+                in_=turned[:].rearrange("p r u j -> p r j u"),
             )
 
-        def quantise(r):
-            x_codes[r] = chunk_pool.tile([P, GROUPS, P], U32, name="codes", align_bytes=64)
-            x_planes[r] = chunk_pool.tile([P, GROUPS, P], U8, name="plane", align_bytes=64)
+        def quantise_duo(duo, g):
             nc.vector.quantize_mx(
-                out=x_codes[r][:].rearrange("p g j -> p (g j)").bitcast(FP8X4),
-                scales=x_planes[r][:].rearrange("p g j -> p (g j)"),
-                in_=x_grouped[r][:],
+                out=x_codes[(duo, g)][:].rearrange("p r j -> p (r j)").bitcast(FP8X4),
+                scales=x_planes[(duo, g)][:].rearrange("p r j -> p (r j)"),
+                in_=x_grouped[(duo, g)][:],
+            )
+
+        def turn_one(duo, g, r):
+            turned = turn_psum.tile([P, PAIRS, P], F32, name="turned")
+            for u in range(PAIRS):
+                nc.tensor.transpose(
+                    turned[:, u, :],
+                    x_rows[(duo, g)][:].bitcast(F32)[:, r, u : P * PAIRS : PAIRS],
+                    identity[:],
+                )
+            nc.scalar.copy(
+                out=x_grouped[(duo, g)][:, P * PACK * r : P * PACK * (r + 1)]
+                .bitcast(F32)
+                .rearrange("p (j u) -> p j u", u=PAIRS),
+                in_=turned[:].rearrange("p u j -> p j u"),
+            )
+
+        def quantise_one(duo, g, r):
+            nc.vector.quantize_mx(
+                out=x_codes[(duo, g)][:, r, :].bitcast(FP8X4),
+                scales=x_planes[(duo, g)][:, r, :],
+                in_=x_grouped[(duo, g)][:, P * PACK * r : P * PACK * (r + 1)],
             )
 
         def spin(count, width):
@@ -108,78 +142,76 @@ def tile_testmmrsmodel_kernel(
                     stop=True,
                 )
 
-        def one_pass(r, g, n):
-            nc.tensor.matmul_mx(
-                out=acc[n][:],
-                lhsT=x_codes[r][:, g, :].bitcast(FP8X4),
-                lhsT_scale=x_planes[r][:, g, :],
-                rhs=w_words[(n, g)][:].bitcast(FP8X4),
-                rhs_scale=w_planes[4 * g : P, N_TILE * n : N_TILE * (n + 1)],
-                start=(g == 0 and r == 0),
-                stop=(g == GROUPS - 1 and r == CHUNKS - 1),
-            )
-
-        def passes(half, n):
-            for g in range(GROUPS):
-                for r in range(HALF * half, HALF * (half + 1)):
-                    one_pass(r, g, n)
-
-        def load_scales(first, last):
-            for quadrant in range(QUADRANTS):
-                top = 32 * quadrant
-                nc.sync.dma_start(
-                    out=w_planes[top : top + 4 * GROUPS, first:last].bitcast(I32),
-                    in_=gate_proj_scales[:, 4 * quadrant : 4 * quadrant + 4, first:last].bitcast(I32),
+        def passes(chunks, g, n):
+            for r in chunks:
+                nc.tensor.matmul_mx(
+                    out=acc[n][:],
+                    lhsT=x_codes[(r // DUO, g)][:, r % DUO, :].bitcast(FP8X4),
+                    lhsT_scale=x_planes[(r // DUO, g)][:, r % DUO, :],
+                    rhs=w_words[(n, g)][:].bitcast(FP8X4),
+                    rhs_scale=w_planes[g][4 * n : P, :],
+                    start=(g == 0 and r == 0),
+                    stop=(g == GROUPS - 1 and r == CHUNKS - 1),
                 )
 
         zeros = keep.tile([P, N_TILE], BF16)
-        nc.vector.memset(zeros[:], 0.0)
+        nc.gpsimd.memset(zeros[:], 0.0)
         identity = keep.tile([P, P], F32)
         make_identity(nc, identity[:])
+        for g in range(GROUPS):
+            w_planes[g] = keep.tile([P, N_TILE], U8, name="w_plane%d" % g, align_bytes=64)
+            nc.vector.memset(w_planes[g][:].bitcast(I32), 0)
         acc = [acc_psum.tile([P, N_TILE], F32, name="acc") for n in range(N_TILES)]
         spin(5, N_TILE)
 
-        w_planes = keep.tile([P, O], U8, align_bytes=64)
-        nc.vector.memset(w_planes[:].bitcast(I32), 0)
-        load_chunks(0)
-        load_w(0, (0,))
-        load_scales(0, N_TILE)
-        load_w(0, (1,))
-        load_scales(N_TILE, O)
-        load_w(1, (0, 1))
-        load_w(2, (0, 1))
-        load_chunks(1)
-        load_w(3, (0, 1))
-
-        sort_words(0)
-        sort_words(1)
-        turn(0)
-        spin(2, 256)
-        sort_words(2)
-        turn(1)
-        spin(2, 256)
-        quantise(0)
-        turn(2)
-        spin(2, 256)
-        quantise(1)
-        turn(3)
-        quantise(2)
-        quantise(3)
-        for g in range(GROUPS):
-            for r in range(HALF - 1):
-                one_pass(r, g, 0)
-        for g in range(GROUPS):
-            one_pass(HALF - 1, g, 0)
-        passes(0, 1)
-        passes(0, 2)
-        for r in range(HALF, CHUNKS):
-            sort_words(r)
-        for r in range(HALF, CHUNKS):
-            turn(r)
-            quantise(r)
-        passes(0, 3)
+        load_x(0, 0)
+        load_scales(0)
+        load_x(1, 0)
+        load_w(0, 0)
+        load_w(1, 0)
+        load_x(2, 0)
+        load_x(3, 0)
+        load_w(2, 0)
+        load_w(3, 0)
+        for duo in range(DUOS):
+            load_x(duo, 1)
+        load_scales(1)
         for n in range(N_TILES):
-            passes(1, n)
-            result = stage.tile([P, N_TILE], F32)
+            load_w(n, 1)
+
+        first = range(0, CHUNKS // 2)
+        second = range(CHUNKS // 2, CHUNKS)
+
+        turn_one(0, 0, 0)
+        turn_one(0, 0, 1)
+        quantise_one(0, 0, 0)
+        turn_one(1, 0, 0)
+        quantise_one(0, 0, 1)
+        turn_one(1, 0, 1)
+        quantise_one(1, 0, 0)
+        quantise_one(1, 0, 1)
+        spin(2, 256)
+        passes(first, 0, 0)
+        passes(first, 0, 1)
+        sort_words(2, 0)
+        sort_words(3, 0)
+        turn_duo(2, 0)
+        turn_duo(3, 0)
+        quantise_duo(2, 0)
+        quantise_duo(3, 0)
+        passes(first, 0, 2)
+        passes(first, 0, 3)
+        passes(second, 0, 0)
+        passes(second, 0, 1)
+        for duo in range(DUOS):
+            sort_words(duo, 1)
+        for duo in range(DUOS):
+            turn_duo(duo, 1)
+            quantise_duo(duo, 1)
+        passes(second, 0, 2)
+        passes(second, 0, 3)
+        for n in range(N_TILES):
+            passes(range(CHUNKS), 1, n)
+            result = out_pool.tile([P, N_TILE], F32, name="result")
             nc.vector.tensor_copy(out=result[:], in_=acc[n][:])
             nc.sync.dma_start(out=out[:, N_TILE * n : N_TILE * (n + 1)], in_=result[:])

@@ -154,7 +154,7 @@ def tile_testmmrsmodel_kernel(
                     stop=(g == GROUPS - 1 and r == CHUNKS - 1),
                 )
 
-        zeros = keep.tile([P, N_TILE], BF16)
+        zeros = keep.tile([P, P], BF16)
         nc.gpsimd.memset(zeros[:], 0.0)
         identity = keep.tile([P, P], F32)
         make_identity(nc, identity[:])
@@ -162,12 +162,12 @@ def tile_testmmrsmodel_kernel(
             w_planes[g] = keep.tile([P, N_TILE], U8, name="w_plane%d" % g, align_bytes=64)
             nc.vector.memset(w_planes[g][:].bitcast(I32), 0)
         acc = [acc_psum.tile([P, N_TILE], F32, name="acc") for n in range(N_TILES)]
-        spin(5, N_TILE)
+        spin(16, P)
 
         load_x(0, 0)
-        load_scales(0)
         load_x(1, 0)
         load_w(0, 0)
+        load_scales(0)
         load_w(1, 0)
         load_x(2, 0)
         load_x(3, 0)
@@ -183,14 +183,16 @@ def tile_testmmrsmodel_kernel(
         second = range(CHUNKS // 2, CHUNKS)
 
         turn_one(0, 0, 0)
+        spin(2, P)
         turn_one(0, 0, 1)
+        spin(2, P)
         quantise_one(0, 0, 0)
         turn_one(1, 0, 0)
+        spin(2, P)
         quantise_one(0, 0, 1)
         turn_one(1, 0, 1)
         quantise_one(1, 0, 0)
         quantise_one(1, 0, 1)
-        spin(2, 256)
         passes(first, 0, 0)
         passes(first, 0, 1)
         sort_words(2, 0)

from contextlib import ExitStack

import concourse.mybir as mybir
from concourse.masks import make_identity

F32 = mybir.dt.float32
BF16 = mybir.dt.bfloat16
I32 = mybir.dt.int32
U32 = mybir.dt.uint32
U8 = mybir.dt.uint8
FP8X4 = mybir.dt.float8_e4m3fn_x4

P = 128
PACK = 4
K_PASS = P * PACK
CHUNKS = 8
DUO = 2
DUOS = CHUNKS // DUO
H = 1024
O = 2048
GROUPS = H // K_PASS
N_TILE = 512
N_TILES = O // N_TILE
PAIRS = PACK // 2
QUADRANTS = 4

FLOPS = 2 * CHUNKS * P * H * O


def tile_testmmrsmodel_kernel(
    tc, hidden_states, gate_proj_words, gate_proj_scales, world_size, out
):
    nc = tc.nc
    assert world_size == CHUNKS

    with ExitStack() as ctx:
        keep = ctx.enter_context(tc.tile_pool(name="keep", bufs=1))
        x_pool = ctx.enter_context(tc.tile_pool(name="x_pool", bufs=DUOS * GROUPS))
        w_pool = ctx.enter_context(tc.tile_pool(name="w_pool", bufs=N_TILES * GROUPS))
        out_pool = ctx.enter_context(tc.tile_pool(name="out_pool", bufs=N_TILES))
        turn_psum = ctx.enter_context(tc.psum_pool(name="turn_psum", bufs=4))
        acc_psum = ctx.enter_context(tc.psum_pool(name="acc_psum", bufs=N_TILES))
        ctx.enter_context(tc.manual_schedule())

        x_rows = {}
        x_sorted = {}
        x_grouped = {}
        x_codes = {}
        x_planes = {}
        w_words = {}
        w_planes = {}

        def load_x(duo, g):
            x_rows[(duo, g)] = x_pool.tile([P, DUO, K_PASS], BF16, name="rows")
            nc.sync.dma_start(
                out=x_rows[(duo, g)][:],
                in_=hidden_states[
                    DUO * duo : DUO * (duo + 1), :, K_PASS * g : K_PASS * (g + 1)
                ].rearrange("r j k -> j r k"),
            )
            x_grouped[(duo, g)] = x_pool.tile(
                [P, DUO * P * PACK], BF16, name="grouped", align_bytes=64
            )
            x_codes[(duo, g)] = x_pool.tile([P, DUO, P], U32, name="codes", align_bytes=64)
            x_planes[(duo, g)] = x_pool.tile([P, DUO, P], U8, name="plane", align_bytes=64)

        def load_w(n, g):
            w_words[(n, g)] = w_pool.tile([P, N_TILE], U32, name="words", align_bytes=64)
            bytes_in_dram = gate_proj_words[g].rearrange("p n t -> p (n t)")
            nc.sync.dma_start(
                out=w_words[(n, g)][:].bitcast(I32),
                in_=bytes_in_dram[:, PACK * N_TILE * n : PACK * N_TILE * (n + 1)].bitcast(I32),
            )

        def load_scales(g):
            for quadrant in range(QUADRANTS):
                top = 32 * quadrant
                nc.sync.dma_start(
                    out=w_planes[g][top : top + 4 * N_TILES, :].bitcast(I32),
                    in_=gate_proj_scales[g, 4 * quadrant : 4 * quadrant + 4, :]
                    .rearrange("s (n c) -> n s c", n=N_TILES)
                    .bitcast(I32),
                )

        def sort_words(duo, g):
            x_sorted[(duo, g)] = x_pool.tile([P, DUO, PAIRS, P], F32, name="sorted_words")
            nc.vector.tensor_copy(
                out=x_sorted[(duo, g)][:],
                in_=x_rows[(duo, g)][:].bitcast(F32).rearrange("j r (p u) -> j r u p", u=PAIRS),
            )

        def turn_duo(duo, g):
            turned = turn_psum.tile([P, DUO, PAIRS, P], F32, name="turned")
            for r in range(DUO):
                for u in range(PAIRS):
                    nc.tensor.transpose(
                        turned[:, r, u, :], x_sorted[(duo, g)][:, r, u, :], identity[:]
                    )
            nc.scalar.copy(
                out=x_grouped[(duo, g)][:]
                .bitcast(F32)
                .rearrange("p (r j u) -> p r j u", r=DUO, u=PAIRS),
                in_=turned[:].rearrange("p r u j -> p r j u"),
            )

        def quantise_duo(duo, g):
            nc.vector.quantize_mx(
                out=x_codes[(duo, g)][:].rearrange("p r j -> p (r j)").bitcast(FP8X4),
                scales=x_planes[(duo, g)][:].rearrange("p r j -> p (r j)"),
                in_=x_grouped[(duo, g)][:],
            )

        def turn_one(duo, g, r):
            turned = turn_psum.tile([P, PAIRS, P], F32, name="turned")
            for u in range(PAIRS):
                nc.tensor.transpose(
                    turned[:, u, :],
                    x_rows[(duo, g)][:].bitcast(F32)[:, r, u : P * PAIRS : PAIRS],
                    identity[:],
                )
            nc.scalar.copy(
                out=x_grouped[(duo, g)][:, P * PACK * r : P * PACK * (r + 1)]
                .bitcast(F32)
                .rearrange("p (j u) -> p j u", u=PAIRS),
                in_=turned[:].rearrange("p u j -> p j u"),
            )

        def quantise_one(duo, g, r):
            nc.vector.quantize_mx(
                out=x_codes[(duo, g)][:, r, :].bitcast(FP8X4),
                scales=x_planes[(duo, g)][:, r, :],
                in_=x_grouped[(duo, g)][:, P * PACK * r : P * PACK * (r + 1)],
            )

        def spin(count, width):
            for i in range(count):
                nc.tensor.matmul(
                    out=acc[N_TILES - 1][:, 0:width],
                    lhsT=zeros[:, 0:P],
                    rhs=zeros[:, 0:width],
                    start=True,
                    stop=True,
                )

        def passes(chunks, g, n):
            for r in chunks:
                nc.tensor.matmul_mx(
                    out=acc[n][:],
                    lhsT=x_codes[(r // DUO, g)][:, r % DUO, :].bitcast(FP8X4),
                    lhsT_scale=x_planes[(r // DUO, g)][:, r % DUO, :],
                    rhs=w_words[(n, g)][:].bitcast(FP8X4),
                    rhs_scale=w_planes[g][4 * n : P, :],
                    start=(g == 0 and r == 0),
                    stop=(g == GROUPS - 1 and r == CHUNKS - 1),
                )

        zeros = keep.tile([P, P], BF16)
        nc.gpsimd.memset(zeros[:], 0.0)
        identity = keep.tile([P, P], F32)
        make_identity(nc, identity[:])
        for g in range(GROUPS):
            w_planes[g] = keep.tile([P, N_TILE], U8, name="w_plane%d" % g, align_bytes=64)
            nc.vector.memset(w_planes[g][:].bitcast(I32), 0)
        acc = [acc_psum.tile([P, N_TILE], F32, name="acc") for n in range(N_TILES)]
        spin(16, P)

        load_x(0, 0)
        load_x(1, 0)
        load_w(0, 0)
        load_scales(0)
        load_w(1, 0)
        load_x(2, 0)
        load_x(3, 0)
        load_w(2, 0)
        load_w(3, 0)
        for duo in range(DUOS):
            load_x(duo, 1)
        load_scales(1)
        for n in range(N_TILES):
            load_w(n, 1)

        first = range(0, CHUNKS // 2)
        second = range(CHUNKS // 2, CHUNKS)

        turn_one(0, 0, 0)
        spin(2, P)
        turn_one(0, 0, 1)
        spin(2, P)
        quantise_one(0, 0, 0)
        turn_one(1, 0, 0)
        spin(2, P)
        quantise_one(0, 0, 1)
        turn_one(1, 0, 1)
        quantise_one(1, 0, 0)
        quantise_one(1, 0, 1)
        passes(first, 0, 0)
        passes(first, 0, 1)
        sort_words(2, 0)
        sort_words(3, 0)
        turn_duo(2, 0)
        turn_duo(3, 0)
        quantise_duo(2, 0)
        quantise_duo(3, 0)
        passes(first, 0, 2)
        passes(first, 0, 3)
        passes(second, 0, 0)
        passes(second, 0, 1)
        for duo in range(DUOS):
            sort_words(duo, 1)
        for duo in range(DUOS):
            turn_duo(duo, 1)
            quantise_duo(duo, 1)
        passes(second, 0, 2)
        passes(second, 0, 3)
        for n in range(N_TILES):
            passes(range(CHUNKS), 1, n)
            result = out_pool.tile([P, N_TILE], F32, name="result")
            nc.vector.tensor_copy(out=result[:], in_=acc[n][:])
            nc.sync.dma_start(out=out[:, N_TILE * n : N_TILE * (n + 1)], in_=result[:])
